import numpy as np
import ml_dtypes


def mxq(x, axis, fmt="e4m3"):
    dtype, down = {"e4m3": (ml_dtypes.float8_e4m3fn, 7), "e5m2": (ml_dtypes.float8_e5m2, 14)}[fmt]
    v = np.moveaxis(np.asarray(x, np.float32).astype(ml_dtypes.bfloat16).astype(np.float64), axis, -1)
    blocks = v.reshape(v.shape[:-1] + (-1, 32))
    amax = np.abs(blocks).max(-1, keepdims=True)
    byte = np.maximum(np.where(amax > 0, np.frexp(amax)[1] - 1 + 127, 0) - down, 1)
    scale = np.exp2(byte - 127.0)
    codes = (blocks / scale).astype(np.float32).astype(dtype).astype(np.float64)
    return np.moveaxis((codes * scale).reshape(v.shape), -1, axis)


WIDE = False


def mx_kscale(k):
    if not WIDE:
        return np.ones(k)
    levels = np.array([10, -10, 5, -5, 0])
    if k % 512:
        return np.exp2(np.random.permutation(np.resize(levels, k // 32))).repeat(32)
    a = np.empty((k // 512, 16))
    for p in range(k // 512):
        a[p, :8] = np.random.permutation(np.resize(levels, 8))
        for g in range(8):
            far = levels[np.abs(levels - a[p, g]) >= 10]
            a[p, g + 8] = far[np.random.randint(len(far))]
    return np.exp2(a.ravel()).repeat(32)


BF16 = ml_dtypes.bfloat16


def bf(x):
    return np.asarray(x, np.float32).astype(BF16)


def f64(x):
    return np.asarray(x).astype(np.float64)


B, N1, N2, D, H, DH = 2, 256, 256, 1024, 8, 128
HD = H * DH
EPS = 1e-6
ROPE_THETA = 10000.0


def split_heads(qkv):
    b, n = qkv.shape[0], qkv.shape[1]
    r = qkv.reshape(b, n, 3, H, DH)
    return tuple(r[:, :, i].transpose(0, 2, 1, 3) for i in range(3))


def rmsnorm(x, gamma):
    inv = 1.0 / np.sqrt(np.mean(np.square(x), axis=-1, keepdims=True) + EPS)
    return x * inv * gamma


def rope(x):
    n, d = x.shape[-2], x.shape[-1]
    inv_freq = 1.0 / ROPE_THETA ** (np.arange(0, d, 2) / d)
    ang = np.arange(n)[:, None] * inv_freq
    cos, sin = np.cos(ang), np.sin(ang)
    x1, x2 = np.split(x, 2, axis=-1)
    return np.concatenate([x1 * cos - x2 * sin, x1 * sin + x2 * cos], axis=-1)


def draw0():
    s1, s2 = mx_kscale(D), mx_kscale(D)
    return {"x_1": bf(np.random.standard_normal((B, N1, D)) * s1),
            "x_2": bf(np.random.standard_normal((B, N2, D)) * s2),
            "w_qkv1": bf(np.random.standard_normal((D, 3 * HD)) / np.sqrt(D) / s1[:, None]),
            "b_qkv1": bf(np.random.standard_normal(3 * HD) * 0.2),
            "w_qkv2": bf(np.random.standard_normal((D, 3 * HD)) / np.sqrt(D) / s2[:, None]),
            "b_qkv2": bf(np.random.standard_normal(3 * HD) * 0.2),
            "qg1": bf(1.2 + 0.1 * np.random.standard_normal(DH)),
            "kg1": bf(1.2 + 0.1 * np.random.standard_normal(DH)),
            "qg2": bf(1.2 + 0.1 * np.random.standard_normal(DH)),
            "kg2": bf(1.2 + 0.1 * np.random.standard_normal(DH))}


def core(x_1, x_2, w_qkv1, b_qkv1, w_qkv2, b_qkv2, qg1, kg1, qg2, kg2):
    qs, ks, vs = [], [], []
    for x, w, b, qg, kg in ((x_1, w_qkv1, b_qkv1, qg1, kg1), (x_2, w_qkv2, b_qkv2, qg2, kg2)):
        qkv = (mxq(f64(x), 2, "e4m3") @ mxq(f64(w), 0, "e4m3")) + f64(b)
        q, k, v = split_heads(qkv)
        qs.append(rmsnorm(q, f64(qg)))
        ks.append(rmsnorm(k, f64(kg)))
        vs.append(v)
    q = np.concatenate(qs, axis=-2)
    k = np.concatenate(ks, axis=-2)
    v = np.concatenate(vs, axis=-2)
    return rope(q), rope(k), v


def e4m3fn_bytes(y):
    return np.clip(np.asarray(y, np.float64), -448.0, 448.0).astype(np.float32).astype(ml_dtypes.float8_e4m3fn).view(np.uint8)


def e4m3fn_values(b):
    return np.asarray(b, np.uint8).view(ml_dtypes.float8_e4m3fn).astype(np.float64)


def setup_inputs():
    d = draw0()
    x0 = np.asarray(d['w_qkv2']).astype(np.float64)
    s = (np.max(np.abs(x0), axis=(1,), keepdims=True) / 448.0).astype(np.float32)
    out = {}
    for k, v in d.items():
        if k == 'w_qkv2':
            out['w_qkv2_bytes'] = e4m3fn_bytes(x0 / s.astype(np.float64))
            out['w_qkv2_scale'] = s
        else:
            out[k] = v
    return out


def reference(x_1, x_2, w_qkv1, b_qkv1, w_qkv2_bytes, w_qkv2_scale, b_qkv2, qg1, kg1, qg2, kg2):
    return core(x_1, x_2, w_qkv1, b_qkv1, e4m3fn_values(w_qkv2_bytes) * w_qkv2_scale.astype(np.float64), b_qkv2, qg1, kg1, qg2, kg2)

@@ -1,0 +1,447 @@
+from contextlib import ExitStack
+
+import concourse.mybir as mybir
+from concourse.masks import make_identity
+
+F32 = mybir.dt.float32
+BF16 = mybir.dt.bfloat16
+I32 = mybir.dt.int32
+U32 = mybir.dt.uint32
+U8 = mybir.dt.uint8
+FP8 = mybir.dt.float8_e4m3fn
+FP8X4 = mybir.dt.float8_e4m3fn_x4
+ALU = mybir.AluOpType
+ACT = mybir.ActivationFunctionType
+
+FLOPS = 2 * 1024 * 1024 * 3072
+
+P = 128
+TWO_PI = 6.283185307179586
+EPS = 1e-6
+PW = 256
+GW = 128
+RUN = 8
+LANE = ((0, 0), (0, 1), (2, 0), (1, 0), (1, 1), (2, 1), (0, 2), (0, 3), (2, 2), (1, 2), (1, 3), (2, 3))
+ORDER = ((0, 0, 0), (0, 0, 1), (1, 0, 0), (1, 0, 1)) + tuple((s, c, sub) for c, sub in LANE[2:] for s in (0, 1))
+FIRST2 = 2
+PIECES = len(ORDER)
+HALVES = ((0, 0), (2, 0), (1, 0), (0, 1), (2, 1), (1, 1))
+
+
+def tile_mmattn_pa_kernel(
+    tc, x_1, x_2, w_qkv1, b_qkv1, w_qkv2_bytes, w_qkv2_scale, b_qkv2, qg1, kg1, qg2, kg2, out_0, out_1, out_2
+):
+    nc = tc.nc
+    outs = (out_0, out_1, out_2)
+    xs_dram = (x_1.flatten_outer_dims(), x_2.flatten_outer_dims())
+    w1v = w_qkv1.rearrange("(g p j) n -> g p j n", g=2, p=P, j=4)
+    w2v = w_qkv2_bytes.rearrange("(g p j) n -> g p j n", g=2, p=P, j=4)
+
+    with ExitStack() as ctx:
+        const = ctx.enter_context(tc.tile_pool(name="const", bufs=1))
+        setup = ctx.enter_context(tc.tile_pool(name="setup", bufs=1))
+        rawp = ctx.enter_context(tc.tile_pool(name="rawp", bufs=3))
+        xraw = ctx.enter_context(tc.tile_pool(name="xraw", bufs=8))
+        stage = ctx.enter_context(tc.tile_pool(name="stage", bufs=3))
+        cpool = ctx.enter_context(tc.tile_pool(name="cpool", bufs=6))
+        work = ctx.enter_context(tc.tile_pool(name="work", bufs=4))
+        small = ctx.enter_context(tc.tile_pool(name="small", bufs=3))
+        outp = ctx.enter_context(tc.tile_pool(name="outp", bufs=8))
+        psum = ctx.enter_context(tc.psum_pool(name="psum", bufs=2))
+
+        warm = const.tile([P, 1], F32, name="warm")
+        nc.vector.memset(warm[:], 0.0)
+        nc.scalar.activation(out=warm[:], in_=warm[:], func=ACT.Sin)
+
+        craw = const.tile([P, P], BF16, name="craw")
+        nc.vector.memset(craw[:], 0.0)
+        nc.sync.dma_start(out=craw[0:16, :], in_=b_qkv1[0:2048].rearrange("(h d) -> h d", d=P))
+        nc.sync.dma_start(out=craw[16:32, :], in_=b_qkv2[0:2048].rearrange("(h d) -> h d", d=P))
+        for r, gain in enumerate((qg1, kg1, qg2, kg2)):
+            nc.sync.dma_start(out=craw[32 + r : 33 + r, :], in_=gain.rearrange("(o d) -> o d", o=1))
+        wsc32 = const.tile([P, 2, 4], F32, name="wsc32")
+        nc.sync.dma_start(out=wsc32[:], in_=w_qkv2_scale.rearrange("(g p j) o -> p g (j o)", g=2, p=P, j=4))
+
+        x_sb = {}
+        raw = {}
+
+        def load_x(s):
+            for tt in range(4):
+                xt_sb = xraw.tile([P, 1024], BF16, name="x_sb", tag="x_sb")
+                nc.sync.dma_start(out=xt_sb[:], in_=xs_dram[s][tt * P : (tt + 1) * P, :])
+                x_sb[(s, tt)] = xt_sb
+
+        def load_w(s, c, sub0, subs):
+            n0 = c * 1024 + sub0 * PW
+            wid = subs * PW
+            if s == 0 and subs == 1:
+                tw = rawp.tile([P, 2, 4, wid], BF16, name="raw1a", tag="raw1a", bufs=2)
+                for g in range(2):
+                    nc.sync.dma_start(out=tw[:, g, :, :], in_=w1v[g][:, :, n0 : n0 + wid])
+            elif s == 0:
+                tw = rawp.tile([P, 2, 4, wid], BF16, name="raw1", tag="raw1")
+                for g in range(2):
+                    nc.sync.dma_start(out=tw[:, g, :, :], in_=w1v[g][:, :, n0 : n0 + wid])
+            else:
+                tw = rawp.tile([P, 2, 4, wid], U8, name="w2bytes", tag="w2bytes")
+                for g in range(2):
+                    nc.sync.dma_start(out=tw[:, g, :, :], in_=w2v[g][:, :, n0 : n0 + wid])
+            for k in range(subs):
+                raw[(s, c, sub0 + k)] = (tw, k * PW)
+
+        bv = []
+
+        def load_bv():
+            for s, bias in enumerate((b_qkv1, b_qkv2)):
+                bvt = const.tile([P, 1024], BF16, name="bv%d" % s)
+                nc.sync.dma_start(out=bvt[:], in_=bias[2048:3072].partition_broadcast(P))
+                bv.append(bvt)
+
+        load_w(0, 0, 0, 1)
+        load_x(0)
+        load_w(0, 0, 1, 1)
+        load_w(1, 0, 0, 2)
+        load_x(1)
+        for c, hf in HALVES[1:3]:
+            load_w(0, c, 2 * hf, 2)
+            load_w(1, c, 2 * hf, 2)
+        load_bv()
+
+        ident = const.tile([P, P], F32, name="ident")
+        make_identity(nc, ident[:])
+        swapm = const.tile([P, P], F32, name="swapm")
+        nc.vector.tensor_copy(out=swapm[:, 0:64], in_=ident[:, 64:128])
+        nc.vector.tensor_copy(out=swapm[:, 64:128], in_=ident[:, 0:64])
+        epst = const.tile([P, 1], F32, name="epst")
+        nc.vector.memset(epst[:], EPS)
+
+        posf = setup.tile([P, 512], F32, name="posf")
+        nc.gpsimd.iota(posf[:], pattern=[[1, 512]], base=0, channel_multiplier=0, allow_small_or_imprecise_dtypes=True)
+        didx = setup.tile([P, 1], I32, name="didx")
+        nc.gpsimd.iota(didx[:], pattern=[[0, 1]], base=0, channel_multiplier=1)
+        bint = setup.tile([P, 7], I32, name="bint")
+        for k in range(7):
+            nc.vector.tensor_scalar(
+                out=bint[:, k : k + 1], in0=didx[:], scalar1=k, scalar2=1,
+                op0=ALU.logical_shift_right, op1=ALU.bitwise_and,
+            )
+        bits = setup.tile([P, 7], F32, name="bits")
+        nc.vector.tensor_copy(out=bits[:], in_=bint[:])
+        nbits = setup.tile([P, 7], F32, name="nbits")
+        nc.vector.tensor_scalar(out=nbits[:], in0=bits[:], scalar1=-1.0, scalar2=1.0, op0=ALU.mult, op1=ALU.add)
+        fac = setup.tile([P, 6], F32, name="fac")
+        for k in range(6):
+            nc.vector.scalar_tensor_tensor(
+                out=fac[:, k : k + 1], in0=bits[:, k : k + 1], scalar=10000.0 ** (-(2.0 ** k) / 64.0),
+                in1=nbits[:, k : k + 1], op0=ALU.mult, op1=ALU.add,
+            )
+        pr3 = setup.tile([P, 3], F32, name="pr3")
+        nc.vector.tensor_tensor(out=pr3[:], in0=fac[:, 0:3], in1=fac[:, 3:6], op=ALU.mult)
+        pr1 = setup.tile([P, 1], F32, name="pr1")
+        nc.vector.tensor_tensor(out=pr1[:], in0=pr3[:, 0:1], in1=pr3[:, 1:2], op=ALU.mult)
+        pr2 = setup.tile([P, 1], F32, name="pr2")
+        nc.vector.tensor_tensor(out=pr2[:], in0=pr1[:], in1=pr3[:, 2:3], op=ALU.mult)
+        hcol = setup.tile([P, 1], F32, name="hcol")
+        nc.vector.tensor_scalar(out=hcol[:], in0=pr2[:], scalar1=1.0 / TWO_PI, scalar2=None, op0=ALU.mult)
+        sgn = setup.tile([P, 1], F32, name="sgn")
+        nc.vector.tensor_scalar(out=sgn[:], in0=bits[:, 6:7], scalar1=-2.0, scalar2=1.0, op0=ALU.mult, op1=ALU.add)
+
+        trigs = []
+
+        def make_trig(s):
+            pos = posf[:, s * 256 : (s + 1) * 256]
+            turn = setup.tile([P, 2, 256], F32, name="turn%d" % s)
+            nc.vector.tensor_scalar(out=turn[:, 0, :], in0=pos, scalar1=hcol[:, 0:1], scalar2=None, op0=ALU.mult)
+            nc.vector.tensor_scalar(out=turn[:, 1, :], in0=pos, scalar1=hcol[:, 0:1], scalar2=0.25, op0=ALU.mult, op1=ALU.add)
+            whole = setup.tile([P, 2, 256], I32, name="whole%d" % s)
+            nc.vector.tensor_copy(out=whole[:], in_=turn[:])
+            nc.vector.tensor_tensor(out=turn[:], in0=turn[:], in1=whole[:], op=ALU.subtract)
+            nc.vector.scalar_tensor_tensor(out=turn[:], in0=turn[:], scalar=0.5, in1=turn[:], op0=ALU.is_gt, op1=ALU.subtract)
+            trig = setup.tile([P, 2, 256], F32, name="trig%d" % s)
+            nc.scalar.activation(out=trig[:], in_=turn[:], func=ACT.Sin, scale=-TWO_PI)
+            trigs.append(trig)
+
+        cst = const.tile([P, 36], F32, name="cst")
+        sgain = const.tile([P, 4], F32, name="sgain")
+
+        def make_cst():
+            c32 = const.tile([P, P], F32, name="c32")
+            nc.gpsimd.tensor_copy(out=c32[:], in_=craw[:])
+            cps = psum.tile([P, 512], F32, name="cps", tag="acc", bufs=4)
+            nc.tensor.transpose(cps[:, 0:P], c32[:], ident[:])
+            nc.vector.tensor_copy(out=cst[:], in_=cps[:, 0:36])
+            nc.vector.tensor_scalar(out=sgain[:], in0=cst[:, 32:36], scalar1=sgn[:, 0:1], scalar2=None, op0=ALU.mult)
+
+        tab = const.tile([P, 4, 2, 2, 256], F32, name="tab")
+
+        def make_tables(s):
+            for c in range(2):
+                ti = 2 * s + c
+                nc.scalar.activation(
+                    out=tab[:, ti, 0, :, :], in_=trigs[s][:, 1, :].unsqueeze(1).to_broadcast([P, 2, 256]),
+                    func=ACT.Copy, scale=cst[:, 32 + ti : 33 + ti],
+                )
+                nc.scalar.activation(
+                    out=tab[:, ti, 1, :, :], in_=trigs[s][:, 0, :].unsqueeze(1).to_broadcast([P, 2, 256]),
+                    func=ACT.Copy, scale=sgain[:, ti : ti + 1],
+                )
+
+        xq = []
+        xsc = []
+
+        def prep_x(s):
+            xg = stage.tile([P, 2, 512, 4], BF16, name="xg", tag="xg", bufs=1, align_bytes=64)
+            xqt = const.tile([P, 2, 512], U32, name="xq%d" % s, align_bytes=64)
+            xst = const.tile([P, 2, 512], U8, name="xsc%d" % s, align_bytes=64)
+            for tt in range(4):
+                words = x_sb[(s, tt)][:].bitcast(F32)
+                xt = psum.tile([P, 512], F32, name="xt", tag="acc", bufs=4)
+                xtv = xt[:].rearrange("p (g u r) -> p g u r", g=2, u=2)
+                for g in range(2):
+                    for u in range(2):
+                        nc.tensor.transpose(xtv[:, g, u, :], words[:, 256 * g + u : 256 * (g + 1) : 2], ident[:])
+                nc.scalar.copy(
+                    out=xg[:, :, tt * P : (tt + 1) * P, :].bitcast(F32),
+                    in_=xtv.rearrange("p g u r -> p g r u"),
+                )
+            for g in range(2):
+                nc.vector.quantize_mx(
+                    out=xqt[:, g, :].bitcast(FP8X4), scales=xst[:, g, :],
+                    in_=xg[:, g, :, :].rearrange("p r j -> p (r j)"),
+                )
+            xq.append(xqt)
+            xsc.append(xst)
+
+        make_trig(0)
+        prep_x(0)
+        make_cst()
+        make_tables(0)
+
+        wide = {}
+        wgt = {}
+        codes = {}
+        csc = {}
+        accs = {}
+        mids = {}
+
+        def widen(i):
+            s, c, sub = ORDER[i]
+            if s == 0:
+                return
+            tw, c0 = raw[(s, c, sub)]
+            wd = stage.tile([P, 2, 4, PW], BF16, name="wide", tag="wide")
+            for g in range(2):
+                for j in range(4):
+                    nc.scalar.activation(
+                        out=wd[:, g, j, :], in_=tw[:, g, j, c0 : c0 + PW].bitcast(FP8),
+                        func=ACT.Copy, scale=wsc32[:, g, j : j + 1],
+                    )
+            wide[i] = wd
+            later_loads(i)
+
+        def later_loads(i):
+            s, c, sub = ORDER[i]
+            if (c, sub) == LANE[1]:
+                load_w(s, HALVES[3][0], 2 * HALVES[3][1], 2)
+            if (c, sub) == LANE[5]:
+                load_w(s, HALVES[4][0], 2 * HALVES[4][1], 2)
+                load_w(s, HALVES[5][0], 2 * HALVES[5][1], 2)
+
+        def inter(i):
+            s, c, sub = ORDER[i]
+            tw, c0 = raw[(s, c, sub)]
+            src = tw[:, :, :, c0 : c0 + PW] if s == 0 else wide[i][:]
+            wg = stage.tile([P, 2, PW, 4], BF16, name="wgt", tag="wgt", bufs=4, align_bytes=64)
+            if s == 0 and i >= FIRST2:
+                for g in range(2):
+                    for w0 in range(0, PW, GW):
+                        nc.gpsimd.tensor_scalar(
+                            out=wg[:, g, w0 : w0 + GW, :].rearrange("p (c i) j -> p c j i", i=RUN),
+                            in0=src[:, g, :, w0 : w0 + GW].rearrange("p j (c i) -> p c j i", i=RUN),
+                            scalar1=1.0, scalar2=0.0, op0=ALU.mult, op1=ALU.add,
+                        )
+            else:
+                for g in range(2):
+                    nc.vector.tensor_copy(
+                        out=wg[:, g, :, :].rearrange("p (c i) j -> p c j i", i=RUN),
+                        in_=src[:, g, :, :].rearrange("p j (c i) -> p c j i", i=RUN),
+                    )
+            wgt[i] = wg
+            if s == 0:
+                later_loads(i)
+
+        def quant(i):
+            codes[i] = cpool.tile([P, 2, PW], U32, name="codes", tag="codes", align_bytes=64)
+            csc[i] = cpool.tile([P, 2, PW], U8, name="csc", tag="csc", align_bytes=64)
+            nc.vector.quantize_mx(
+                out=codes[i][:].rearrange("p g w -> p (g w)").bitcast(FP8X4),
+                scales=csc[i][:].rearrange("p g w -> p (g w)"),
+                in_=wgt[i][:].rearrange("p g w j -> p (g w j)"),
+            )
+
+        def mx(i, halves=(0, 1)):
+            ci = i
+            s, c, sub = ORDER[i]
+            c0 = 0
+            got = accs.setdefault(i, [])
+            for half in halves:
+                acc = psum.tile([P, 512], F32, name="acc", tag="acc", bufs=4)
+                if c < 2:
+                    h0 = c0 + half * P
+                    for g in range(2):
+                        nc.tensor.matmul_mx(
+                            out=acc[:],
+                            lhsT=codes[ci][:, g, h0 : h0 + P].bitcast(FP8X4), lhsT_scale=csc[ci][:, g, h0 : h0 + P],
+                            rhs=xq[s][:, g, :].bitcast(FP8X4), rhs_scale=xsc[s][:, g, :],
+                            start=(g == 0), stop=(g == 1),
+                        )
+                else:
+                    for t in range(2):
+                        t0 = (2 * half + t) * P
+                        for g in range(2):
+                            nc.tensor.matmul_mx(
+                                out=acc[:, t * PW : (t + 1) * PW],
+                                lhsT=xq[s][:, g, t0 : t0 + P].bitcast(FP8X4), lhsT_scale=xsc[s][:, g, t0 : t0 + P],
+                                rhs=codes[ci][:, g, c0 : c0 + PW].bitcast(FP8X4), rhs_scale=csc[ci][:, g, c0 : c0 + PW],
+                                start=(g == 0), stop=(g == 1),
+                            )
+                got.append(acc)
+
+        def v_out(i):
+            s, c, sub = ORDER[i]
+            for b in range(2):
+                vo = outp.tile([P, 2, PW], F32, name="vo", tag="vo")
+                nc.vector.tensor_tensor(
+                    out=vo[:], in0=accs[i][b][:].rearrange("p (t n) -> p t n", t=2),
+                    in1=bv[s][:, sub * PW : (sub + 1) * PW].unsqueeze(1).to_broadcast([P, 2, PW]), op=ALU.add,
+                )
+                for t in range(2):
+                    n0 = s * 256 + t * P
+                    nc.sync.dma_start(
+                        out=out_2[b, 2 * sub : 2 * sub + 2, n0 : n0 + P, :].rearrange("h p d -> p h d"),
+                        in_=vo[:, t, :].rearrange("p (h d) -> p h d", h=2),
+                    )
+
+        def bias_col(i, half):
+            s, c, sub = ORDER[i]
+            col = 16 * s + 8 * c + 2 * sub + half
+            return cst[:, col : col + 1]
+
+        sqs = {}
+        uws = {}
+        sqts = {}
+        rots = {}
+        invs = {}
+
+        def squares(i):
+            got = []
+            for half in range(2):
+                sq = work.tile([P, 512], F32, name="sq", tag="sq")
+                nc.scalar.activation(out=sq[:], in_=accs[i][half][:], func=ACT.Square, bias=bias_col(i, half), scale=1.0)
+                got.append(sq)
+            sqs[i] = got
+
+        def products(i):
+            s, c, sub = ORDER[i]
+            got = []
+            for half in range(2):
+                uw = work.tile([P, 2, 512], F32, name="uw", tag="uw")
+                nc.vector.scalar_tensor_tensor(
+                    out=uw[:], in0=accs[i][half][:].unsqueeze(1).to_broadcast([P, 2, 512]), scalar=bias_col(i, half),
+                    in1=tab[:, 2 * s + c, :, :, :].rearrange("p f b n -> p f (b n)"), op0=ALU.add, op1=ALU.mult,
+                )
+                got.append(uw)
+            uws[i] = got
+
+        def turn_squares(i, halves=(0, 1)):
+            got = sqts.setdefault(i, [])
+            for half in halves:
+                sqt = psum.tile([P, 4, P], F32, name="sqt", tag="sqt", bufs=2)
+                for tt in range(4):
+                    nc.tensor.transpose(sqt[:, tt, :], sqs[i][half][:, tt * P : (tt + 1) * P], ident[:])
+                got.append(sqt)
+
+        def sums(i):
+            ssum = small.tile([P, 8], F32, name="ssum", tag="ssum")
+            nc.vector.tensor_reduce(out=ssum[:, 0:4], in_=sqts[i][0][:], axis=mybir.AxisListType.X, op=ALU.add)
+            for tt in range(4):
+                junk = work.tile([P, P], F32, name="junk", tag="junk")
+                nc.scalar.activation(
+                    out=junk[:], in_=sqts[i][1][:, tt, :], func=ACT.Copy, accum_out=ssum[:, 4 + tt : 5 + tt],
+                )
+            inv = small.tile([P, 8], F32, name="inv", tag="inv")
+            nc.scalar.activation(out=inv[:], in_=ssum[:], func=ACT.Abs_reciprocal_sqrt, bias=epst[:, 0:1], scale=1.0 / 128.0)
+            invs[i] = inv
+
+        def rotate(i, halves=(0, 1)):
+            got = rots.setdefault(i, [])
+            for half in halves:
+                uw = uws[i][half]
+                rot = psum.tile([P, 4, P], F32, name="rot", tag="rot", bufs=2)
+                for tt in range(4):
+                    nc.tensor.matmul(
+                        out=rot[:, tt, :], lhsT=uw[:, 0, tt * P : (tt + 1) * P], rhs=ident[:],
+                        start=True, stop=False, is_transpose=True,
+                    )
+                    nc.tensor.matmul(
+                        out=rot[:, tt, :], lhsT=uw[:, 1, tt * P : (tt + 1) * P], rhs=swapm[:],
+                        start=False, stop=True, is_transpose=True,
+                    )
+                got.append(rot)
+
+        def finish(i):
+            s, c, sub = ORDER[i]
+            for half in range(2):
+                ot = outp.tile([P, 4, P], F32, name="ot", tag="ot")
+                for tt in range(4):
+                    nc.scalar.activation(
+                        out=ot[:, tt, :], in_=rots[i][half][:, tt, :], func=ACT.Copy,
+                        scale=invs[i][:, 4 * half + tt : 4 * half + tt + 1],
+                    )
+                hh = 2 * sub + half
+                for b in range(2):
+                    nc.sync.dma_start(
+                        out=outs[c][b, hh, s * 256 : (s + 1) * 256, :].rearrange("(t p) d -> p t d", p=P),
+                        in_=ot[:, 2 * b : 2 * b + 2, :],
+                    )
+
+        def is_piece(i):
+            return 0 <= i < PIECES
+
+        def is_qk(i):
+            return is_piece(i) and ORDER[i][1] < 2
+
+        ctx.enter_context(tc.manual_schedule(engines={mybir.EngineType.PE}))
+        for tau in range(-4, PIECES + 1):
+            if is_qk(tau):
+                squares(tau)
+            if is_qk(tau - 1):
+                sums(tau - 1)
+                rotate(tau - 1, (0,))
+            if is_piece(tau + 1) and tau + 1 != FIRST2:
+                mx(tau + 1, (0,))
+            if is_qk(tau - 1):
+                rotate(tau - 1, (1,))
+            if is_qk(tau):
+                products(tau)
+                turn_squares(tau, (0,))
+            elif is_piece(tau):
+                v_out(tau)
+            if is_piece(tau + 1) and tau + 1 != FIRST2:
+                mx(tau + 1, (1,))
+            if is_qk(tau):
+                turn_squares(tau, (1,))
+            if is_qk(tau - 1):
+                finish(tau - 1)
+            if tau == 0:
+                make_trig(1)
+            if tau + 1 == FIRST2:
+                prep_x(1)
+                make_tables(1)
+                mx(FIRST2)
+            if is_piece(tau + 2):
+                quant(tau + 2)
+            if is_piece(tau + 3):
+                inter(tau + 3)
+            if is_piece(tau + 4):
+                widen(tau + 4)

@@ -177,13 +177,13 @@ def tile_mmattn_pa_kernel(
         def make_tables(s):
             for c in range(2):
                 ti = 2 * s + c
-                nc.scalar.activation(
-                    out=tab[:, ti, 0, :, :], in_=trigs[s][:, 1, :].unsqueeze(1).to_broadcast([P, 2, 256]),
-                    func=ACT.Copy, scale=cst[:, 32 + ti : 33 + ti],
+                nc.vector.tensor_scalar(
+                    out=tab[:, ti, 0, :, :], in0=trigs[s][:, 1, :].unsqueeze(1).to_broadcast([P, 2, 256]),
+                    scalar1=cst[:, 32 + ti : 33 + ti], scalar2=None, op0=ALU.mult,
                 )
-                nc.scalar.activation(
-                    out=tab[:, ti, 1, :, :], in_=trigs[s][:, 0, :].unsqueeze(1).to_broadcast([P, 2, 256]),
-                    func=ACT.Copy, scale=sgain[:, ti : ti + 1],
+                nc.vector.tensor_scalar(
+                    out=tab[:, ti, 1, :, :], in0=trigs[s][:, 0, :].unsqueeze(1).to_broadcast([P, 2, 256]),
+                    scalar1=sgain[:, ti : ti + 1], scalar2=None, op0=ALU.mult,
                 )
 
         xq = []

@@ -19,7 +19,7 @@ P = 128
 TWO_PI = 6.283185307179586
 EPS = 1e-6
 PW = 256
-GW = 128
+BANKS = {"acc": 4, "sqt": 2, "rot": 2}
 RUN = 8
 LANE = ((0, 0), (0, 1), (2, 0), (1, 0), (1, 1), (2, 1), (0, 2), (0, 3), (2, 2), (1, 2), (1, 3), (2, 3))
 ORDER = ((0, 0, 0), (0, 0, 1), (1, 0, 0), (1, 0, 1)) + tuple((s, c, sub) for c, sub in LANE[2:] for s in (0, 1))
@@ -53,15 +53,8 @@ def tile_mmattn_pa_kernel(
         nc.vector.memset(warm[:], 0.0)
         nc.scalar.activation(out=warm[:], in_=warm[:], func=ACT.Sin)
 
-        craw = const.tile([P, P], BF16, name="craw")
+        craw = const.tile([P, PW], BF16, name="craw")
         nc.vector.memset(craw[:], 0.0)
-        nc.sync.dma_start(out=craw[0:16, :], in_=b_qkv1[0:2048].rearrange("(h d) -> h d", d=P))
-        nc.sync.dma_start(out=craw[16:32, :], in_=b_qkv2[0:2048].rearrange("(h d) -> h d", d=P))
-        for r, gain in enumerate((qg1, kg1, qg2, kg2)):
-            nc.sync.dma_start(out=craw[32 + r : 33 + r, :], in_=gain.rearrange("(o d) -> o d", o=1))
-        wsc32 = const.tile([P, 2, 4], F32, name="wsc32")
-        nc.sync.dma_start(out=wsc32[:], in_=w_qkv2_scale.rearrange("(g p j) o -> p g (j o)", g=2, p=P, j=4))
-
         x_sb = {}
         raw = {}
 
@@ -100,6 +93,12 @@ def tile_mmattn_pa_kernel(
         load_w(0, 0, 0, 1)
         load_x(0)
         load_w(0, 0, 1, 1)
+        for s, bias in enumerate((b_qkv1, b_qkv2)):
+            nc.sync.dma_start(out=craw[8 * s : 8 * s + 8, :], in_=bias[0:2048].rearrange("(m n) -> m n", n=PW))
+        for r, gain in enumerate((qg1, kg1, qg2, kg2)):
+            nc.sync.dma_start(out=craw[32 + r : 33 + r, 0:P], in_=gain.rearrange("(o d) -> o d", o=1))
+        wsc32 = const.tile([P, 2, 4], F32, name="wsc32")
+        nc.sync.dma_start(out=wsc32[:], in_=w_qkv2_scale.rearrange("(g p j) o -> p g (j o)", g=2, p=P, j=4))
         load_w(1, 0, 0, 2)
         load_x(1)
         for c, hf in HALVES[1:3]:
@@ -109,9 +108,6 @@ def tile_mmattn_pa_kernel(
 
         ident = const.tile([P, P], F32, name="ident")
         make_identity(nc, ident[:])
-        swapm = const.tile([P, P], F32, name="swapm")
-        nc.vector.tensor_copy(out=swapm[:, 0:64], in_=ident[:, 64:128])
-        nc.vector.tensor_copy(out=swapm[:, 64:128], in_=ident[:, 0:64])
         epst = const.tile([P, 1], F32, name="epst")
         nc.vector.memset(epst[:], EPS)
 
@@ -119,15 +115,15 @@ def tile_mmattn_pa_kernel(
         nc.gpsimd.iota(posf[:], pattern=[[1, 512]], base=0, channel_multiplier=0, allow_small_or_imprecise_dtypes=True)
         didx = setup.tile([P, 1], I32, name="didx")
         nc.gpsimd.iota(didx[:], pattern=[[0, 1]], base=0, channel_multiplier=1)
-        bint = setup.tile([P, 7], I32, name="bint")
-        for k in range(7):
+        bint = setup.tile([P, 6], I32, name="bint")
+        for k in range(6):
             nc.vector.tensor_scalar(
                 out=bint[:, k : k + 1], in0=didx[:], scalar1=k, scalar2=1,
                 op0=ALU.logical_shift_right, op1=ALU.bitwise_and,
             )
-        bits = setup.tile([P, 7], F32, name="bits")
+        bits = setup.tile([P, 6], F32, name="bits")
         nc.vector.tensor_copy(out=bits[:], in_=bint[:])
-        nbits = setup.tile([P, 7], F32, name="nbits")
+        nbits = setup.tile([P, 6], F32, name="nbits")
         nc.vector.tensor_scalar(out=nbits[:], in0=bits[:], scalar1=-1.0, scalar2=1.0, op0=ALU.mult, op1=ALU.add)
         fac = setup.tile([P, 6], F32, name="fac")
         for k in range(6):
@@ -143,8 +139,6 @@ def tile_mmattn_pa_kernel(
         nc.vector.tensor_tensor(out=pr2[:], in0=pr1[:], in1=pr3[:, 2:3], op=ALU.mult)
         hcol = setup.tile([P, 1], F32, name="hcol")
         nc.vector.tensor_scalar(out=hcol[:], in0=pr2[:], scalar1=1.0 / TWO_PI, scalar2=None, op0=ALU.mult)
-        sgn = setup.tile([P, 1], F32, name="sgn")
-        nc.vector.tensor_scalar(out=sgn[:], in0=bits[:, 6:7], scalar1=-2.0, scalar2=1.0, op0=ALU.mult, op1=ALU.add)
 
         trigs = []
 
@@ -161,41 +155,42 @@ def tile_mmattn_pa_kernel(
             nc.scalar.activation(out=trig[:], in_=turn[:], func=ACT.Sin, scale=-TWO_PI)
             trigs.append(trig)
 
-        cst = const.tile([P, 36], F32, name="cst")
-        sgain = const.tile([P, 4], F32, name="sgain")
+        cst = const.tile([P, 2, 36], F32, name="cst")
+        ngain = const.tile([P, 4], F32, name="ngain")
 
         def make_cst():
-            c32 = const.tile([P, P], F32, name="c32")
-            nc.gpsimd.tensor_copy(out=c32[:], in_=craw[:])
-            cps = psum.tile([P, 512], F32, name="cps", tag="acc", bufs=4)
-            nc.tensor.transpose(cps[:, 0:P], c32[:], ident[:])
-            nc.vector.tensor_copy(out=cst[:], in_=cps[:, 0:36])
-            nc.vector.tensor_scalar(out=sgain[:], in0=cst[:, 32:36], scalar1=sgn[:, 0:1], scalar2=None, op0=ALU.mult)
+            c32 = const.tile([P, 2, 2, 64], F32, name="c32")
+            nc.gpsimd.tensor_copy(out=c32[:], in_=craw[:].rearrange("p (h f d) -> p f h d", h=2, f=2))
+            for h in range(2):
+                nc.gpsimd.tensor_copy(out=c32[32:64, :, h, :], in_=craw[32:64, 0:P].rearrange("p (f d) -> p f d", f=2))
+            cps = psum.tile([P, 2, P], F32, name="cps", tag="acc", bufs=BANKS["acc"])
+            for f in range(2):
+                nc.tensor.transpose(cps[:, f, :], c32[:, f, :, :].rearrange("p h d -> p (h d)"), ident[:])
+            nc.vector.tensor_copy(out=cst[:], in_=cps[:, :, 0:36])
+            nc.vector.tensor_scalar(out=ngain[:], in0=cst[:, 1, 32:36], scalar1=-1.0, scalar2=None, op0=ALU.mult)
 
         tab = const.tile([P, 4, 2, 2, 256], F32, name="tab")
 
         def make_tables(s):
             for c in range(2):
                 ti = 2 * s + c
-                nc.vector.tensor_scalar(
-                    out=tab[:, ti, 0, :, :], in0=trigs[s][:, 1, :].unsqueeze(1).to_broadcast([P, 2, 256]),
-                    scalar1=cst[:, 32 + ti : 33 + ti], scalar2=None, op0=ALU.mult,
-                )
-                nc.vector.tensor_scalar(
-                    out=tab[:, ti, 1, :, :], in0=trigs[s][:, 0, :].unsqueeze(1).to_broadcast([P, 2, 256]),
-                    scalar1=sgain[:, ti : ti + 1], scalar2=None, op0=ALU.mult,
-                )
+                sinr, cosr = trigs[s][:, 0, :], trigs[s][:, 1, :]
+                for f, r, src, col in (
+                    (0, 0, cosr, cst[:, 0, 32 + ti : 33 + ti]), (0, 1, sinr, cst[:, 0, 32 + ti : 33 + ti]),
+                    (1, 0, sinr, ngain[:, ti : ti + 1]), (1, 1, cosr, cst[:, 1, 32 + ti : 33 + ti]),
+                ):
+                    nc.vector.tensor_scalar(out=tab[:, ti, f, r, :], in0=src, scalar1=col, scalar2=None, op0=ALU.mult)
 
         xq = []
         xsc = []
 
-        def prep_x(s):
+        def prep_x(s, tags):
             xg = stage.tile([P, 2, 512, 4], BF16, name="xg", tag="xg", bufs=1, align_bytes=64)
             xqt = const.tile([P, 2, 512], U32, name="xq%d" % s, align_bytes=64)
             xst = const.tile([P, 2, 512], U8, name="xsc%d" % s, align_bytes=64)
             for tt in range(4):
                 words = x_sb[(s, tt)][:].bitcast(F32)
-                xt = psum.tile([P, 512], F32, name="xt", tag="acc", bufs=4)
+                xt = psum.tile([P, 512], F32, name="xt", tag=tags[tt % 2], bufs=BANKS[tags[tt % 2]])
                 xtv = xt[:].rearrange("p (g u r) -> p g u r", g=2, u=2)
                 for g in range(2):
                     for u in range(2):
@@ -213,7 +208,7 @@ def tile_mmattn_pa_kernel(
             xsc.append(xst)
 
         make_trig(0)
-        prep_x(0)
+        prep_x(0, ("acc", "acc"))
         make_cst()
         make_tables(0)
 
@@ -222,7 +217,6 @@ def tile_mmattn_pa_kernel(
         codes = {}
         csc = {}
         accs = {}
-        mids = {}
 
         def widen(i):
             s, c, sub = ORDER[i]
@@ -252,20 +246,27 @@ def tile_mmattn_pa_kernel(
             tw, c0 = raw[(s, c, sub)]
             src = tw[:, :, :, c0 : c0 + PW] if s == 0 else wide[i][:]
             wg = stage.tile([P, 2, PW, 4], BF16, name="wgt", tag="wgt", bufs=4, align_bytes=64)
-            if s == 0 and i >= FIRST2:
-                for g in range(2):
-                    for w0 in range(0, PW, GW):
-                        nc.gpsimd.tensor_scalar(
-                            out=wg[:, g, w0 : w0 + GW, :].rearrange("p (c i) j -> p c j i", i=RUN),
-                            in0=src[:, g, :, w0 : w0 + GW].rearrange("p j (c i) -> p c j i", i=RUN),
-                            scalar1=1.0, scalar2=0.0, op0=ALU.mult, op1=ALU.add,
+            for g in range(2):
+                for h in range(2):
+                    sr = src[:, g, :, h * P : (h + 1) * P]
+                    if s == 0 and i >= FIRST2:
+                        if c < 2:
+                            ds = wg[:, g, :, :].rearrange("p (f h d) j -> p h f d j", f=2, h=2)[:, h, :, :, :]
+                            sr = sr.rearrange("p j (f d) -> p f d j", f=2)
+                        else:
+                            ds = wg[:, g, h * P : (h + 1) * P, :]
+                            sr = sr.rearrange("p j d -> p d j")
+                        nc.gpsimd.tensor_scalar(out=ds, in0=sr, scalar1=1.0, scalar2=0.0, op0=ALU.mult, op1=ALU.add)
+                    elif c < 2:
+                        nc.vector.tensor_copy(
+                            out=wg[:, g, :, :].rearrange("p (f h c i) j -> p h f c j i", f=2, h=2, i=RUN)[:, h, :, :, :, :],
+                            in_=sr.rearrange("p j (f c i) -> p f c j i", f=2, i=RUN),
                         )
-            else:
-                for g in range(2):
-                    nc.vector.tensor_copy(
-                        out=wg[:, g, :, :].rearrange("p (c i) j -> p c j i", i=RUN),
-                        in_=src[:, g, :, :].rearrange("p j (c i) -> p c j i", i=RUN),
-                    )
+                    else:
+                        nc.scalar.copy(
+                            out=wg[:, g, h * P : (h + 1) * P, :].rearrange("p (c i) j -> p c j i", i=RUN),
+                            in_=sr.rearrange("p j (c i) -> p c j i", i=RUN),
+                        )
             wgt[i] = wg
             if s == 0:
                 later_loads(i)
@@ -285,7 +286,7 @@ def tile_mmattn_pa_kernel(
             c0 = 0
             got = accs.setdefault(i, [])
             for half in halves:
-                acc = psum.tile([P, 512], F32, name="acc", tag="acc", bufs=4)
+                acc = psum.tile([P, 512], F32, name="acc", tag="acc", bufs=BANKS["acc"])
                 if c < 2:
                     h0 = c0 + half * P
                     for g in range(2):
@@ -324,8 +325,8 @@ def tile_mmattn_pa_kernel(
 
         def bias_col(i, half):
             s, c, sub = ORDER[i]
-            col = 16 * s + 8 * c + 2 * sub + half
-            return cst[:, col : col + 1]
+            row = 8 * s + 4 * c + sub
+            return cst[:, half, row : row + 1]
 
         sqs = {}
         uws = {}
@@ -346,63 +347,61 @@ def tile_mmattn_pa_kernel(
             got = []
             for half in range(2):
                 uw = work.tile([P, 2, 512], F32, name="uw", tag="uw")
-                nc.vector.scalar_tensor_tensor(
-                    out=uw[:], in0=accs[i][half][:].unsqueeze(1).to_broadcast([P, 2, 512]), scalar=bias_col(i, half),
-                    in1=tab[:, 2 * s + c, :, :, :].rearrange("p f b n -> p f (b n)"), op0=ALU.add, op1=ALU.mult,
-                )
+                for b in range(2):
+                    cols = slice(b * 256, (b + 1) * 256)
+                    nc.vector.scalar_tensor_tensor(
+                        out=uw[:, :, cols], in0=accs[i][half][:, cols].unsqueeze(1).to_broadcast([P, 2, 256]), scalar=bias_col(i, half),
+                        in1=tab[:, 2 * s + c, half, :, :], op0=ALU.add, op1=ALU.mult,
+                    )
                 got.append(uw)
             uws[i] = got
 
-        def turn_squares(i, halves=(0, 1)):
-            got = sqts.setdefault(i, [])
-            for half in halves:
-                sqt = psum.tile([P, 4, P], F32, name="sqt", tag="sqt", bufs=2)
-                for tt in range(4):
-                    nc.tensor.transpose(sqt[:, tt, :], sqs[i][half][:, tt * P : (tt + 1) * P], ident[:])
-                got.append(sqt)
+        def turn_squares(i):
+            sqt = psum.tile([P, 4, P], F32, name="sqt", tag="sqt", bufs=BANKS["sqt"])
+            for tt in range(4):
+                for half in range(2):
+                    nc.tensor.matmul(
+                        out=sqt[:, tt, :], lhsT=sqs[i][half][:, tt * P : (tt + 1) * P], rhs=ident[:],
+                        start=(half == 0), stop=(half == 1), is_transpose=True,
+                    )
+            sqts[i] = sqt
 
         def sums(i):
             ssum = small.tile([P, 8], F32, name="ssum", tag="ssum")
-            nc.vector.tensor_reduce(out=ssum[:, 0:4], in_=sqts[i][0][:], axis=mybir.AxisListType.X, op=ALU.add)
-            for tt in range(4):
-                junk = work.tile([P, P], F32, name="junk", tag="junk")
-                nc.scalar.activation(
-                    out=junk[:], in_=sqts[i][1][:, tt, :], func=ACT.Copy, accum_out=ssum[:, 4 + tt : 5 + tt],
-                )
+            nc.vector.tensor_reduce(
+                out=ssum[:], in_=sqts[i][:].rearrange("p t (h d) -> p (t h) d", h=2), axis=mybir.AxisListType.X, op=ALU.add
+            )
             inv = small.tile([P, 8], F32, name="inv", tag="inv")
             nc.scalar.activation(out=inv[:], in_=ssum[:], func=ACT.Abs_reciprocal_sqrt, bias=epst[:, 0:1], scale=1.0 / 128.0)
             invs[i] = inv
 
-        def rotate(i, halves=(0, 1)):
+        def rotate(i, bats=(0, 1)):
             got = rots.setdefault(i, [])
-            for half in halves:
-                uw = uws[i][half]
-                rot = psum.tile([P, 4, P], F32, name="rot", tag="rot", bufs=2)
-                for tt in range(4):
-                    nc.tensor.matmul(
-                        out=rot[:, tt, :], lhsT=uw[:, 0, tt * P : (tt + 1) * P], rhs=ident[:],
-                        start=True, stop=False, is_transpose=True,
-                    )
-                    nc.tensor.matmul(
-                        out=rot[:, tt, :], lhsT=uw[:, 1, tt * P : (tt + 1) * P], rhs=swapm[:],
-                        start=False, stop=True, is_transpose=True,
-                    )
+            for b in bats:
+                rot = psum.tile([P, 2, 2, P], F32, name="rot", tag="rot", bufs=BANKS["rot"])
+                for t in range(2):
+                    tok = (2 * b + t) * P
+                    for r in range(2):
+                        for half in range(2):
+                            nc.tensor.matmul(
+                                out=rot[:, t, r, :], lhsT=uws[i][half][:, r, tok : tok + P], rhs=ident[:],
+                                start=(half == 0), stop=(half == 1), is_transpose=True,
+                            )
                 got.append(rot)
 
         def finish(i):
             s, c, sub = ORDER[i]
-            for half in range(2):
-                ot = outp.tile([P, 4, P], F32, name="ot", tag="ot")
-                for tt in range(4):
-                    nc.scalar.activation(
-                        out=ot[:, tt, :], in_=rots[i][half][:, tt, :], func=ACT.Copy,
-                        scale=invs[i][:, 4 * half + tt : 4 * half + tt + 1],
-                    )
-                hh = 2 * sub + half
-                for b in range(2):
+            for b in range(2):
+                ot = outp.tile([P, 2, 2, 2, 64], F32, name="ot", tag="ot")
+                for h in range(2):
+                    for t in range(2):
+                        nc.scalar.activation(
+                            out=ot[:, h, t, :, :], in_=rots[i][b][:, t, :, h * 64 : (h + 1) * 64], func=ACT.Copy,
+                            scale=invs[i][:, 4 * b + 2 * t + h : 4 * b + 2 * t + h + 1],
+                        )
                     nc.sync.dma_start(
-                        out=outs[c][b, hh, s * 256 : (s + 1) * 256, :].rearrange("(t p) d -> p t d", p=P),
-                        in_=ot[:, 2 * b : 2 * b + 2, :],
+                        out=outs[c][b, 2 * sub + h, s * 256 : (s + 1) * 256, :].rearrange("(t p) d -> p t d", p=P),
+                        in_=ot[:, h, :, :, :].rearrange("p t r d -> p t (r d)"),
                     )
 
         def is_piece(i):
@@ -418,27 +417,25 @@ def tile_mmattn_pa_kernel(
             if is_qk(tau - 1):
                 sums(tau - 1)
                 rotate(tau - 1, (0,))
-            if is_piece(tau + 1) and tau + 1 != FIRST2:
+            if is_piece(tau + 1):
                 mx(tau + 1, (0,))
             if is_qk(tau - 1):
                 rotate(tau - 1, (1,))
             if is_qk(tau):
                 products(tau)
-                turn_squares(tau, (0,))
             elif is_piece(tau):
                 v_out(tau)
-            if is_piece(tau + 1) and tau + 1 != FIRST2:
+            if is_piece(tau + 1):
                 mx(tau + 1, (1,))
             if is_qk(tau):
-                turn_squares(tau, (1,))
+                turn_squares(tau)
             if is_qk(tau - 1):
                 finish(tau - 1)
             if tau == 0:
                 make_trig(1)
-            if tau + 1 == FIRST2:
-                prep_x(1)
                 make_tables(1)
-                mx(FIRST2)
+            if tau == -1:
+                prep_x(1, ("rot", "sqt"))
             if is_piece(tau + 2):
                 quant(tau + 2)
             if is_piece(tau + 3):

@@ -92,13 +92,13 @@ def tile_mmattn_pa_kernel(
 
         load_w(0, 0, 0, 1)
         load_x(0)
-        load_w(0, 0, 1, 1)
         for s, bias in enumerate((b_qkv1, b_qkv2)):
             nc.sync.dma_start(out=craw[8 * s : 8 * s + 8, :], in_=bias[0:2048].rearrange("(m n) -> m n", n=PW))
         for r, gain in enumerate((qg1, kg1, qg2, kg2)):
             nc.sync.dma_start(out=craw[32 + r : 33 + r, 0:P], in_=gain.rearrange("(o d) -> o d", o=1))
         wsc32 = const.tile([P, 2, 4], F32, name="wsc32")
         nc.sync.dma_start(out=wsc32[:], in_=w_qkv2_scale.rearrange("(g p j) o -> p g (j o)", g=2, p=P, j=4))
+        load_w(0, 0, 1, 1)
         load_w(1, 0, 0, 2)
         load_x(1)
         for c, hf in HALVES[1:3]:
@@ -106,6 +106,8 @@ def tile_mmattn_pa_kernel(
             load_w(1, c, 2 * hf, 2)
         load_bv()
 
+        didx = setup.tile([P, 1], I32, name="didx")
+        nc.gpsimd.iota(didx[:], pattern=[[0, 1]], base=0, channel_multiplier=1)
         ident = const.tile([P, P], F32, name="ident")
         make_identity(nc, ident[:])
         epst = const.tile([P, 1], F32, name="epst")
@@ -113,8 +115,6 @@ def tile_mmattn_pa_kernel(
 
         posf = setup.tile([P, 512], F32, name="posf")
         nc.gpsimd.iota(posf[:], pattern=[[1, 512]], base=0, channel_multiplier=0, allow_small_or_imprecise_dtypes=True)
-        didx = setup.tile([P, 1], I32, name="didx")
-        nc.gpsimd.iota(didx[:], pattern=[[0, 1]], base=0, channel_multiplier=1)
         bint = setup.tile([P, 6], I32, name="bint")
         for k in range(6):
             nc.vector.tensor_scalar(
@@ -140,20 +140,20 @@ def tile_mmattn_pa_kernel(
         hcol = setup.tile([P, 1], F32, name="hcol")
         nc.vector.tensor_scalar(out=hcol[:], in0=pr2[:], scalar1=1.0 / TWO_PI, scalar2=None, op0=ALU.mult)
 
-        trigs = []
-
-        def make_trig(s):
-            pos = posf[:, s * 256 : (s + 1) * 256]
-            turn = setup.tile([P, 2, 256], F32, name="turn%d" % s)
-            nc.vector.tensor_scalar(out=turn[:, 0, :], in0=pos, scalar1=hcol[:, 0:1], scalar2=None, op0=ALU.mult)
-            nc.vector.tensor_scalar(out=turn[:, 1, :], in0=pos, scalar1=hcol[:, 0:1], scalar2=0.25, op0=ALU.mult, op1=ALU.add)
-            whole = setup.tile([P, 2, 256], I32, name="whole%d" % s)
-            nc.vector.tensor_copy(out=whole[:], in_=turn[:])
-            nc.vector.tensor_tensor(out=turn[:], in0=turn[:], in1=whole[:], op=ALU.subtract)
-            nc.vector.scalar_tensor_tensor(out=turn[:], in0=turn[:], scalar=0.5, in1=turn[:], op0=ALU.is_gt, op1=ALU.subtract)
-            trig = setup.tile([P, 2, 256], F32, name="trig%d" % s)
-            nc.scalar.activation(out=trig[:], in_=turn[:], func=ACT.Sin, scale=-TWO_PI)
-            trigs.append(trig)
+        turn = setup.tile([P, 2, 512], F32, name="turn")
+        nc.vector.tensor_scalar(out=turn[:, 0, :], in0=posf[:], scalar1=hcol[:, 0:1], scalar2=None, op0=ALU.mult)
+        whole = setup.tile([P, 512], I32, name="whole")
+        nc.vector.tensor_copy(out=whole[:], in_=turn[:, 0, :])
+        nc.vector.tensor_tensor(out=turn[:, 0, :], in0=turn[:, 0, :], in1=whole[:], op=ALU.subtract)
+        nc.vector.scalar_tensor_tensor(
+            out=turn[:, 0, :], in0=turn[:, 0, :], scalar=0.5, in1=turn[:, 0, :], op0=ALU.is_gt, op1=ALU.subtract
+        )
+        nc.vector.tensor_scalar(out=turn[:, 1, :], in0=turn[:, 0, :], scalar1=-0.25, scalar2=None, op0=ALU.add)
+        nc.vector.scalar_tensor_tensor(
+            out=turn[:, 1, :], in0=turn[:, 1, :], scalar=-0.5, in1=turn[:, 1, :], op0=ALU.is_lt, op1=ALU.add
+        )
+        trig = setup.tile([P, 2, 512], F32, name="trig")
+        nc.scalar.activation(out=trig[:], in_=turn[:], func=ACT.Sin, scale=-TWO_PI)
 
         cst = const.tile([P, 2, 36], F32, name="cst")
         ngain = const.tile([P, 4], F32, name="ngain")
@@ -174,12 +174,15 @@ def tile_mmattn_pa_kernel(
         def make_tables(s):
             for c in range(2):
                 ti = 2 * s + c
-                sinr, cosr = trigs[s][:, 0, :], trigs[s][:, 1, :]
+                sinr, cosr = trig[:, 0, s * 256 : (s + 1) * 256], trig[:, 1, s * 256 : (s + 1) * 256]
                 for f, r, src, col in (
                     (0, 0, cosr, cst[:, 0, 32 + ti : 33 + ti]), (0, 1, sinr, cst[:, 0, 32 + ti : 33 + ti]),
                     (1, 0, sinr, ngain[:, ti : ti + 1]), (1, 1, cosr, cst[:, 1, 32 + ti : 33 + ti]),
                 ):
-                    nc.vector.tensor_scalar(out=tab[:, ti, f, r, :], in0=src, scalar1=col, scalar2=None, op0=ALU.mult)
+                    if s == 0:
+                        nc.vector.tensor_scalar(out=tab[:, ti, f, r, :], in0=src, scalar1=col, scalar2=None, op0=ALU.mult)
+                    else:
+                        nc.gpsimd.tensor_scalar(out=tab[:, ti, f, r, :], in0=src, scalar1=col, scalar2=0.0, op0=ALU.mult, op1=ALU.add)
 
         xq = []
         xsc = []
@@ -207,10 +210,10 @@ def tile_mmattn_pa_kernel(
             xq.append(xqt)
             xsc.append(xst)
 
-        make_trig(0)
         prep_x(0, ("acc", "acc"))
         make_cst()
         make_tables(0)
+        make_tables(1)
 
         wide = {}
         wgt = {}
@@ -263,10 +266,7 @@ def tile_mmattn_pa_kernel(
                             in_=sr.rearrange("p j (f c i) -> p f c j i", f=2, i=RUN),
                         )
                     else:
-                        nc.scalar.copy(
-                            out=wg[:, g, h * P : (h + 1) * P, :].rearrange("p (c i) j -> p c j i", i=RUN),
-                            in_=sr.rearrange("p j (c i) -> p c j i", i=RUN),
-                        )
+                        nc.scalar.copy(out=wg[:, g, h * P : (h + 1) * P, :], in_=sr.rearrange("p j d -> p d j"))
             wgt[i] = wg
             if s == 0:
                 later_loads(i)
@@ -431,9 +431,6 @@ def tile_mmattn_pa_kernel(
                 turn_squares(tau)
             if is_qk(tau - 1):
                 finish(tau - 1)
-            if tau == 0:
-                make_trig(1)
-                make_tables(1)
             if tau == -1:
                 prep_x(1, ("rot", "sqt"))
             if is_piece(tau + 2):

@@ -116,9 +116,9 @@ def tile_mmattn_pa_kernel(
         posf = setup.tile([P, 512], F32, name="posf")
         nc.gpsimd.iota(posf[:], pattern=[[1, 512]], base=0, channel_multiplier=0, allow_small_or_imprecise_dtypes=True)
         bint = setup.tile([P, 6], I32, name="bint")
-        for k in range(6):
+        for k, bit in enumerate((0, 1, 2, 4, 5, 6)):
             nc.vector.tensor_scalar(
-                out=bint[:, k : k + 1], in0=didx[:], scalar1=k, scalar2=1,
+                out=bint[:, k : k + 1], in0=didx[:], scalar1=bit, scalar2=1,
                 op0=ALU.logical_shift_right, op1=ALU.bitwise_and,
             )
         bits = setup.tile([P, 6], F32, name="bits")
@@ -159,13 +159,14 @@ def tile_mmattn_pa_kernel(
         ngain = const.tile([P, 4], F32, name="ngain")
 
         def make_cst():
-            c32 = const.tile([P, 2, 2, 64], F32, name="c32")
-            nc.gpsimd.tensor_copy(out=c32[:], in_=craw[:].rearrange("p (h f d) -> p f h d", h=2, f=2))
+            c32 = const.tile([P, 2 * P], F32, name="c32")
             for h in range(2):
-                nc.gpsimd.tensor_copy(out=c32[32:64, :, h, :], in_=craw[32:64, 0:P].rearrange("p (f d) -> p f d", f=2))
+                ds = c32[:].rearrange("p (c h i) -> p h c i", h=2, i=RUN)[:, h, :, :]
+                nc.gpsimd.tensor_copy(out=ds, in_=craw[:, h * P : (h + 1) * P].rearrange("p (c i) -> p c i", i=RUN))
+                nc.gpsimd.tensor_copy(out=ds[32:64, :, :], in_=craw[32:64, 0:P].rearrange("p (c i) -> p c i", i=RUN))
             cps = psum.tile([P, 2, P], F32, name="cps", tag="acc", bufs=BANKS["acc"])
             for f in range(2):
-                nc.tensor.transpose(cps[:, f, :], c32[:, f, :, :].rearrange("p h d -> p (h d)"), ident[:])
+                nc.tensor.transpose(cps[:, f, :], c32[:, f * P : (f + 1) * P], ident[:])
             nc.vector.tensor_copy(out=cst[:], in_=cps[:, :, 0:36])
             nc.vector.tensor_scalar(out=ngain[:], in0=cst[:, 1, 32:36], scalar1=-1.0, scalar2=None, op0=ALU.mult)
 
@@ -250,23 +251,22 @@ def tile_mmattn_pa_kernel(
             src = tw[:, :, :, c0 : c0 + PW] if s == 0 else wide[i][:]
             wg = stage.tile([P, 2, PW, 4], BF16, name="wgt", tag="wgt", bufs=4, align_bytes=64)
             for g in range(2):
+                if s == 1 and c < 2 or i < FIRST2:
+                    nc.vector.tensor_copy(
+                        out=wg[:, g, :, :].rearrange("p (c h i) j -> p h c j i", h=2, i=RUN),
+                        in_=src[:, g, :, :].rearrange("p j (h c i) -> p h c j i", h=2, i=RUN),
+                    )
+                    continue
                 for h in range(2):
-                    sr = src[:, g, :, h * P : (h + 1) * P]
-                    if s == 0 and i >= FIRST2:
-                        if c < 2:
-                            ds = wg[:, g, :, :].rearrange("p (f h d) j -> p h f d j", f=2, h=2)[:, h, :, :, :]
-                            sr = sr.rearrange("p j (f d) -> p f d j", f=2)
-                        else:
-                            ds = wg[:, g, h * P : (h + 1) * P, :]
-                            sr = sr.rearrange("p j d -> p d j")
-                        nc.gpsimd.tensor_scalar(out=ds, in0=sr, scalar1=1.0, scalar2=0.0, op0=ALU.mult, op1=ALU.add)
-                    elif c < 2:
-                        nc.vector.tensor_copy(
-                            out=wg[:, g, :, :].rearrange("p (f h c i) j -> p h f c j i", f=2, h=2, i=RUN)[:, h, :, :, :, :],
-                            in_=sr.rearrange("p j (f c i) -> p f c j i", f=2, i=RUN),
-                        )
+                    sr = src[:, g, :, h * P : (h + 1) * P].rearrange("p j (c i) -> p c i j", i=RUN)
+                    if c < 2:
+                        ds = wg[:, g, :, :].rearrange("p (c h i) j -> p h c i j", h=2, i=RUN)[:, h, :, :, :]
                     else:
-                        nc.scalar.copy(out=wg[:, g, h * P : (h + 1) * P, :], in_=sr.rearrange("p j d -> p d j"))
+                        ds = wg[:, g, h * P : (h + 1) * P, :].rearrange("p (c i) j -> p c i j", i=RUN)
+                    if s == 0:
+                        nc.gpsimd.tensor_scalar(out=ds, in0=sr, scalar1=1.0, scalar2=0.0, op0=ALU.mult, op1=ALU.add)
+                    else:
+                        nc.scalar.copy(out=ds, in_=sr)
             wgt[i] = wg
             if s == 0:
                 later_loads(i)
@@ -369,7 +369,8 @@ def tile_mmattn_pa_kernel(
         def sums(i):
             ssum = small.tile([P, 8], F32, name="ssum", tag="ssum")
             nc.vector.tensor_reduce(
-                out=ssum[:], in_=sqts[i][:].rearrange("p t (h d) -> p (t h) d", h=2), axis=mybir.AxisListType.X, op=ALU.add
+                out=ssum[:].rearrange("p (t h) -> p t h", h=2), in_=sqts[i][:].rearrange("p t (c h i) -> p t h c i", h=2, i=RUN),
+                axis=mybir.AxisListType.XY, op=ALU.add,
             )
             inv = small.tile([P, 8], F32, name="inv", tag="inv")
             nc.scalar.activation(out=inv[:], in_=ssum[:], func=ACT.Abs_reciprocal_sqrt, bias=epst[:, 0:1], scale=1.0 / 128.0)
@@ -392,16 +393,17 @@ def tile_mmattn_pa_kernel(
         def finish(i):
             s, c, sub = ORDER[i]
             for b in range(2):
-                ot = outp.tile([P, 2, 2, 2, 64], F32, name="ot", tag="ot")
+                ot = outp.tile([P, 2, 2, P], F32, name="ot", tag="ot")
                 for h in range(2):
                     for t in range(2):
                         nc.scalar.activation(
-                            out=ot[:, h, t, :, :], in_=rots[i][b][:, t, :, h * 64 : (h + 1) * 64], func=ACT.Copy,
+                            out=ot[:, h, t, :].rearrange("p (c i) -> p c i", i=RUN),
+                            in_=rots[i][b][:, t, :, :].rearrange("p r (c h i) -> p h (r c) i", h=2, i=RUN)[:, h, :, :], func=ACT.Copy,
                             scale=invs[i][:, 4 * b + 2 * t + h : 4 * b + 2 * t + h + 1],
                         )
                     nc.sync.dma_start(
                         out=outs[c][b, 2 * sub + h, s * 256 : (s + 1) * 256, :].rearrange("(t p) d -> p t d", p=P),
-                        in_=ot[:, h, :, :, :].rearrange("p t r d -> p t (r d)"),
+                        in_=ot[:, h, :, :],
                     )
 
         def is_piece(i):

@@ -19,7 +19,7 @@ P = 128
 TWO_PI = 6.283185307179586
 EPS = 1e-6
 PW = 256
-BANKS = {"acc": 4, "sqt": 2, "rot": 2}
+BANKS = {"acc": 4, "sqt": 1, "rot": 3}
 RUN = 8
 LANE = ((0, 0), (0, 1), (2, 0), (1, 0), (1, 1), (2, 1), (0, 2), (0, 3), (2, 2), (1, 2), (1, 3), (2, 3))
 ORDER = ((0, 0, 0), (0, 0, 1), (1, 0, 0), (1, 0, 1)) + tuple((s, c, sub) for c, sub in LANE[2:] for s in (0, 1))
@@ -266,7 +266,7 @@ def tile_mmattn_pa_kernel(
                     if s == 0:
                         nc.gpsimd.tensor_scalar(out=ds, in0=sr, scalar1=1.0, scalar2=0.0, op0=ALU.mult, op1=ALU.add)
                     else:
-                        nc.scalar.copy(out=ds, in_=sr)
+                        nc.scalar.copy(out=ds.rearrange("p c i j -> p c j i"), in_=sr.rearrange("p c i j -> p c j i"))
             wgt[i] = wg
             if s == 0:
                 later_loads(i)
@@ -434,7 +434,7 @@ def tile_mmattn_pa_kernel(
             if is_qk(tau - 1):
                 finish(tau - 1)
             if tau == -1:
-                prep_x(1, ("rot", "sqt"))
+                prep_x(1, ("rot", "rot"))
             if is_piece(tau + 2):
                 quant(tau + 2)
             if is_piece(tau + 3):

@@ -33,7 +33,7 @@ def tile_mmattn_pa_kernel(
 ):
     nc = tc.nc
     outs = (out_0, out_1, out_2)
-    xs_dram = (x_1.flatten_outer_dims(), x_2.flatten_outer_dims())
+    xs_dram = [x.rearrange("b (r t) d -> b t r d", t=2) for x in (x_1, x_2)]
     w1v = w_qkv1.rearrange("(g p j) n -> g p j n", g=2, p=P, j=4)
     w2v = w_qkv2_bytes.rearrange("(g p j) n -> g p j n", g=2, p=P, j=4)
 
@@ -61,7 +61,7 @@ def tile_mmattn_pa_kernel(
         def load_x(s):
             for tt in range(4):
                 xt_sb = xraw.tile([P, 1024], BF16, name="x_sb", tag="x_sb")
-                nc.sync.dma_start(out=xt_sb[:], in_=xs_dram[s][tt * P : (tt + 1) * P, :])
+                nc.sync.dma_start(out=xt_sb[:], in_=xs_dram[s][tt // 2, tt % 2])
                 x_sb[(s, tt)] = xt_sb
 
         def load_w(s, c, sub0, subs):
@@ -114,7 +114,7 @@ def tile_mmattn_pa_kernel(
         nc.vector.memset(epst[:], EPS)
 
         posf = setup.tile([P, 512], F32, name="posf")
-        nc.gpsimd.iota(posf[:], pattern=[[1, 512]], base=0, channel_multiplier=0, allow_small_or_imprecise_dtypes=True)
+        nc.gpsimd.iota(posf[:], pattern=[[256, 2], [1, 2], [2, 128]], base=0, channel_multiplier=0, allow_small_or_imprecise_dtypes=True)
         bint = setup.tile([P, 6], I32, name="bint")
         for k, bit in enumerate((0, 1, 2, 4, 5, 6)):
             nc.vector.tensor_scalar(
@@ -311,17 +311,20 @@ def tile_mmattn_pa_kernel(
         def v_out(i):
             s, c, sub = ORDER[i]
             for b in range(2):
-                vo = outp.tile([P, 2, PW], F32, name="vo", tag="vo")
+                vo = outp.tile([P, 2, 2, P], F32, name="vo", tag="vo")
                 nc.vector.tensor_tensor(
-                    out=vo[:], in0=accs[i][b][:].rearrange("p (t n) -> p t n", t=2),
-                    in1=bv[s][:, sub * PW : (sub + 1) * PW].unsqueeze(1).to_broadcast([P, 2, PW]), op=ALU.add,
+                    out=vo[:].rearrange("p h t d -> p t h d"), in0=accs[i][b][:].rearrange("p (t h d) -> p t h d", t=2, h=2),
+                    in1=bv[s][:, sub * PW : (sub + 1) * PW].rearrange("p (h d) -> p h d", h=2).unsqueeze(1).to_broadcast([P, 2, 2, P]),
+                    op=ALU.add,
                 )
-                for t in range(2):
-                    n0 = s * 256 + t * P
-                    nc.sync.dma_start(
-                        out=out_2[b, 2 * sub : 2 * sub + 2, n0 : n0 + P, :].rearrange("h p d -> p h d"),
-                        in_=vo[:, t, :].rearrange("p (h d) -> p h d", h=2),
-                    )
+                store(out_2, b, i, vo)
+
+        def store(out, b, i, tile):
+            s, c, sub = ORDER[i]
+            nc.sync.dma_start(
+                out=out[b, 2 * sub : 2 * sub + 2, s * 256 : (s + 1) * 256, :].rearrange("h (p t) d -> p h (t d)", t=2),
+                in_=tile[:].rearrange("p h t d -> p h (t d)"),
+            )
 
         def bias_col(i, half):
             s, c, sub = ORDER[i]
@@ -401,10 +404,7 @@ def tile_mmattn_pa_kernel(
                             in_=rots[i][b][:, t, :, :].rearrange("p r (c h i) -> p h (r c) i", h=2, i=RUN)[:, h, :, :], func=ACT.Copy,
                             scale=invs[i][:, 4 * b + 2 * t + h : 4 * b + 2 * t + h + 1],
                         )
-                    nc.sync.dma_start(
-                        out=outs[c][b, 2 * sub + h, s * 256 : (s + 1) * 256, :].rearrange("(t p) d -> p t d", p=P),
-                        in_=ot[:, h, :, :],
-                    )
+                store(outs[c], b, i, ot)
 
         def is_piece(i):
             return 0 <= i < PIECES

from contextlib import ExitStack

import concourse.mybir as mybir
from concourse.masks import make_identity

F32 = mybir.dt.float32
BF16 = mybir.dt.bfloat16
I32 = mybir.dt.int32
U32 = mybir.dt.uint32
U8 = mybir.dt.uint8
FP8 = mybir.dt.float8_e4m3fn
FP8X4 = mybir.dt.float8_e4m3fn_x4
ALU = mybir.AluOpType
ACT = mybir.ActivationFunctionType

FLOPS = 2 * 1024 * 1024 * 3072

P = 128
TWO_PI = 6.283185307179586
EPS = 1e-6
PW = 256
BANKS = {"acc": 4, "sqt": 1, "rot": 3}
RUN = 8
LANE = ((0, 0), (0, 1), (2, 0), (1, 0), (1, 1), (2, 1), (0, 2), (0, 3), (2, 2), (1, 2), (1, 3), (2, 3))
ORDER = ((0, 0, 0), (0, 0, 1), (1, 0, 0), (1, 0, 1)) + tuple((s, c, sub) for c, sub in LANE[2:] for s in (0, 1))
FIRST2 = 2
PIECES = len(ORDER)
HALVES = ((0, 0), (2, 0), (1, 0), (0, 1), (2, 1), (1, 1))


def tile_mmattn_pa_kernel(
    tc, x_1, x_2, w_qkv1, b_qkv1, w_qkv2_bytes, w_qkv2_scale, b_qkv2, qg1, kg1, qg2, kg2, out_0, out_1, out_2
):
    nc = tc.nc
    outs = (out_0, out_1, out_2)
    xs_dram = [x.rearrange("b (r t) d -> b t r d", t=2) for x in (x_1, x_2)]
    w1v = w_qkv1.rearrange("(g p j) n -> g p j n", g=2, p=P, j=4)
    w2v = w_qkv2_bytes.rearrange("(g p j) n -> g p j n", g=2, p=P, j=4)

    with ExitStack() as ctx:
        const = ctx.enter_context(tc.tile_pool(name="const", bufs=1))
        setup = ctx.enter_context(tc.tile_pool(name="setup", bufs=1))
        rawp = ctx.enter_context(tc.tile_pool(name="rawp", bufs=3))
        xraw = ctx.enter_context(tc.tile_pool(name="xraw", bufs=8))
        stage = ctx.enter_context(tc.tile_pool(name="stage", bufs=3))
        cpool = ctx.enter_context(tc.tile_pool(name="cpool", bufs=6))
        work = ctx.enter_context(tc.tile_pool(name="work", bufs=4))
        small = ctx.enter_context(tc.tile_pool(name="small", bufs=3))
        outp = ctx.enter_context(tc.tile_pool(name="outp", bufs=8))
        psum = ctx.enter_context(tc.psum_pool(name="psum", bufs=2))

        warm = const.tile([P, 1], F32, name="warm")
        nc.vector.memset(warm[:], 0.0)
        nc.scalar.activation(out=warm[:], in_=warm[:], func=ACT.Sin)

        craw = const.tile([P, PW], BF16, name="craw")
        nc.vector.memset(craw[:], 0.0)
        x_sb = {}
        raw = {}

        def load_x(s):
            for tt in range(4):
                xt_sb = xraw.tile([P, 1024], BF16, name="x_sb", tag="x_sb")
                nc.sync.dma_start(out=xt_sb[:], in_=xs_dram[s][tt // 2, tt % 2])
                x_sb[(s, tt)] = xt_sb

        def load_w(s, c, sub0, subs):
            n0 = c * 1024 + sub0 * PW
            wid = subs * PW
            if s == 0 and subs == 1:
                tw = rawp.tile([P, 2, 4, wid], BF16, name="raw1a", tag="raw1a", bufs=2)
                for g in range(2):
                    nc.sync.dma_start(out=tw[:, g, :, :], in_=w1v[g][:, :, n0 : n0 + wid])
            elif s == 0:
                tw = rawp.tile([P, 2, 4, wid], BF16, name="raw1", tag="raw1")
                for g in range(2):
                    nc.sync.dma_start(out=tw[:, g, :, :], in_=w1v[g][:, :, n0 : n0 + wid])
            else:
                tw = rawp.tile([P, 2, 4, wid], U8, name="w2bytes", tag="w2bytes")
                for g in range(2):
                    nc.sync.dma_start(out=tw[:, g, :, :], in_=w2v[g][:, :, n0 : n0 + wid])
            for k in range(subs):
                raw[(s, c, sub0 + k)] = (tw, k * PW)

        bv = []

        def load_bv():
            for s, bias in enumerate((b_qkv1, b_qkv2)):
                bvt = const.tile([P, 1024], BF16, name="bv%d" % s)
                nc.sync.dma_start(out=bvt[:], in_=bias[2048:3072].partition_broadcast(P))
                bv.append(bvt)

        load_w(0, 0, 0, 1)
        load_x(0)
        for s, bias in enumerate((b_qkv1, b_qkv2)):
            nc.sync.dma_start(out=craw[8 * s : 8 * s + 8, :], in_=bias[0:2048].rearrange("(m n) -> m n", n=PW))
        for r, gain in enumerate((qg1, kg1, qg2, kg2)):
            nc.sync.dma_start(out=craw[32 + r : 33 + r, 0:P], in_=gain.rearrange("(o d) -> o d", o=1))
        wsc32 = const.tile([P, 2, 4], F32, name="wsc32")
        nc.sync.dma_start(out=wsc32[:], in_=w_qkv2_scale.rearrange("(g p j) o -> p g (j o)", g=2, p=P, j=4))
        load_w(0, 0, 1, 1)
        load_w(1, 0, 0, 2)
        load_x(1)
        for c, hf in HALVES[1:3]:
            load_w(0, c, 2 * hf, 2)
            load_w(1, c, 2 * hf, 2)
        load_bv()

        didx = setup.tile([P, 1], I32, name="didx")
        nc.gpsimd.iota(didx[:], pattern=[[0, 1]], base=0, channel_multiplier=1)
        ident = const.tile([P, P], F32, name="ident")
        make_identity(nc, ident[:])
        epst = const.tile([P, 1], F32, name="epst")
        nc.vector.memset(epst[:], EPS)

        posf = setup.tile([P, 512], F32, name="posf")
        nc.gpsimd.iota(posf[:], pattern=[[256, 2], [1, 2], [2, 128]], base=0, channel_multiplier=0, allow_small_or_imprecise_dtypes=True)
        bint = setup.tile([P, 6], I32, name="bint")
        for k, bit in enumerate((0, 1, 2, 4, 5, 6)):
            nc.vector.tensor_scalar(
                out=bint[:, k : k + 1], in0=didx[:], scalar1=bit, scalar2=1,
                op0=ALU.logical_shift_right, op1=ALU.bitwise_and,
            )
        bits = setup.tile([P, 6], F32, name="bits")
        nc.vector.tensor_copy(out=bits[:], in_=bint[:])
        nbits = setup.tile([P, 6], F32, name="nbits")
        nc.vector.tensor_scalar(out=nbits[:], in0=bits[:], scalar1=-1.0, scalar2=1.0, op0=ALU.mult, op1=ALU.add)
        fac = setup.tile([P, 6], F32, name="fac")
        for k in range(6):
            nc.vector.scalar_tensor_tensor(
                out=fac[:, k : k + 1], in0=bits[:, k : k + 1], scalar=10000.0 ** (-(2.0 ** k) / 64.0),
                in1=nbits[:, k : k + 1], op0=ALU.mult, op1=ALU.add,
            )
        pr3 = setup.tile([P, 3], F32, name="pr3")
        nc.vector.tensor_tensor(out=pr3[:], in0=fac[:, 0:3], in1=fac[:, 3:6], op=ALU.mult)
        pr1 = setup.tile([P, 1], F32, name="pr1")
        nc.vector.tensor_tensor(out=pr1[:], in0=pr3[:, 0:1], in1=pr3[:, 1:2], op=ALU.mult)
        pr2 = setup.tile([P, 1], F32, name="pr2")
        nc.vector.tensor_tensor(out=pr2[:], in0=pr1[:], in1=pr3[:, 2:3], op=ALU.mult)
        hcol = setup.tile([P, 1], F32, name="hcol")
        nc.vector.tensor_scalar(out=hcol[:], in0=pr2[:], scalar1=1.0 / TWO_PI, scalar2=None, op0=ALU.mult)

        turn = setup.tile([P, 2, 512], F32, name="turn")
        nc.vector.tensor_scalar(out=turn[:, 0, :], in0=posf[:], scalar1=hcol[:, 0:1], scalar2=None, op0=ALU.mult)
        whole = setup.tile([P, 512], I32, name="whole")
        nc.vector.tensor_copy(out=whole[:], in_=turn[:, 0, :])
        nc.vector.tensor_tensor(out=turn[:, 0, :], in0=turn[:, 0, :], in1=whole[:], op=ALU.subtract)
        nc.vector.scalar_tensor_tensor(
            out=turn[:, 0, :], in0=turn[:, 0, :], scalar=0.5, in1=turn[:, 0, :], op0=ALU.is_gt, op1=ALU.subtract
        )
        nc.vector.tensor_scalar(out=turn[:, 1, :], in0=turn[:, 0, :], scalar1=-0.25, scalar2=None, op0=ALU.add)
        nc.vector.scalar_tensor_tensor(
            out=turn[:, 1, :], in0=turn[:, 1, :], scalar=-0.5, in1=turn[:, 1, :], op0=ALU.is_lt, op1=ALU.add
        )
        trig = setup.tile([P, 2, 512], F32, name="trig")
        nc.scalar.activation(out=trig[:], in_=turn[:], func=ACT.Sin, scale=-TWO_PI)

        cst = const.tile([P, 2, 36], F32, name="cst")
        ngain = const.tile([P, 4], F32, name="ngain")

        def make_cst():
            c32 = const.tile([P, 2 * P], F32, name="c32")
            for h in range(2):
                ds = c32[:].rearrange("p (c h i) -> p h c i", h=2, i=RUN)[:, h, :, :]
                nc.gpsimd.tensor_copy(out=ds, in_=craw[:, h * P : (h + 1) * P].rearrange("p (c i) -> p c i", i=RUN))
                nc.gpsimd.tensor_copy(out=ds[32:64, :, :], in_=craw[32:64, 0:P].rearrange("p (c i) -> p c i", i=RUN))
            cps = psum.tile([P, 2, P], F32, name="cps", tag="acc", bufs=BANKS["acc"])
            for f in range(2):
                nc.tensor.transpose(cps[:, f, :], c32[:, f * P : (f + 1) * P], ident[:])
            nc.vector.tensor_copy(out=cst[:], in_=cps[:, :, 0:36])
            nc.vector.tensor_scalar(out=ngain[:], in0=cst[:, 1, 32:36], scalar1=-1.0, scalar2=None, op0=ALU.mult)

        tab = const.tile([P, 4, 2, 2, 256], F32, name="tab")

        def make_tables(s):
            for c in range(2):
                ti = 2 * s + c
                sinr, cosr = trig[:, 0, s * 256 : (s + 1) * 256], trig[:, 1, s * 256 : (s + 1) * 256]
                for f, r, src, col in (
                    (0, 0, cosr, cst[:, 0, 32 + ti : 33 + ti]), (0, 1, sinr, cst[:, 0, 32 + ti : 33 + ti]),
                    (1, 0, sinr, ngain[:, ti : ti + 1]), (1, 1, cosr, cst[:, 1, 32 + ti : 33 + ti]),
                ):
                    if s == 0:
                        nc.vector.tensor_scalar(out=tab[:, ti, f, r, :], in0=src, scalar1=col, scalar2=None, op0=ALU.mult)
                    else:
                        nc.gpsimd.tensor_scalar(out=tab[:, ti, f, r, :], in0=src, scalar1=col, scalar2=0.0, op0=ALU.mult, op1=ALU.add)

        xq = []
        xsc = []

        def prep_x(s, tags):
            xg = stage.tile([P, 2, 512, 4], BF16, name="xg", tag="xg", bufs=1, align_bytes=64)
            xqt = const.tile([P, 2, 512], U32, name="xq%d" % s, align_bytes=64)
            xst = const.tile([P, 2, 512], U8, name="xsc%d" % s, align_bytes=64)
            for tt in range(4):
                words = x_sb[(s, tt)][:].bitcast(F32)
                xt = psum.tile([P, 512], F32, name="xt", tag=tags[tt % 2], bufs=BANKS[tags[tt % 2]])
                xtv = xt[:].rearrange("p (g u r) -> p g u r", g=2, u=2)
                for g in range(2):
                    for u in range(2):
                        nc.tensor.transpose(xtv[:, g, u, :], words[:, 256 * g + u : 256 * (g + 1) : 2], ident[:])
                nc.scalar.copy(
                    out=xg[:, :, tt * P : (tt + 1) * P, :].bitcast(F32),
                    in_=xtv.rearrange("p g u r -> p g r u"),
                )
            for g in range(2):
                nc.vector.quantize_mx(
                    out=xqt[:, g, :].bitcast(FP8X4), scales=xst[:, g, :],
                    in_=xg[:, g, :, :].rearrange("p r j -> p (r j)"),
                )
            xq.append(xqt)
            xsc.append(xst)

        prep_x(0, ("acc", "acc"))
        make_cst()
        make_tables(0)
        make_tables(1)

        wide = {}
        wgt = {}
        codes = {}
        csc = {}
        accs = {}

        def widen(i):
            s, c, sub = ORDER[i]
            if s == 0:
                return
            tw, c0 = raw[(s, c, sub)]
            wd = stage.tile([P, 2, 4, PW], BF16, name="wide", tag="wide")
            for g in range(2):
                for j in range(4):
                    nc.scalar.activation(
                        out=wd[:, g, j, :], in_=tw[:, g, j, c0 : c0 + PW].bitcast(FP8),
                        func=ACT.Copy, scale=wsc32[:, g, j : j + 1],
                    )
            wide[i] = wd
            later_loads(i)

        def later_loads(i):
            s, c, sub = ORDER[i]
            if (c, sub) == LANE[1]:
                load_w(s, HALVES[3][0], 2 * HALVES[3][1], 2)
            if (c, sub) == LANE[5]:
                load_w(s, HALVES[4][0], 2 * HALVES[4][1], 2)
                load_w(s, HALVES[5][0], 2 * HALVES[5][1], 2)

        def inter(i):
            s, c, sub = ORDER[i]
            tw, c0 = raw[(s, c, sub)]
            src = tw[:, :, :, c0 : c0 + PW] if s == 0 else wide[i][:]
            wg = stage.tile([P, 2, PW, 4], BF16, name="wgt", tag="wgt", bufs=4, align_bytes=64)
            for g in range(2):
                if s == 1 and c < 2 or i < FIRST2:
                    nc.vector.tensor_copy(
                        out=wg[:, g, :, :].rearrange("p (c h i) j -> p h c j i", h=2, i=RUN),
                        in_=src[:, g, :, :].rearrange("p j (h c i) -> p h c j i", h=2, i=RUN),
                    )
                    continue
                for h in range(2):
                    sr = src[:, g, :, h * P : (h + 1) * P].rearrange("p j (c i) -> p c i j", i=RUN)
                    if c < 2:
                        ds = wg[:, g, :, :].rearrange("p (c h i) j -> p h c i j", h=2, i=RUN)[:, h, :, :, :]
                    else:
                        ds = wg[:, g, h * P : (h + 1) * P, :].rearrange("p (c i) j -> p c i j", i=RUN)
                    if s == 0:
                        nc.gpsimd.tensor_scalar(out=ds, in0=sr, scalar1=1.0, scalar2=0.0, op0=ALU.mult, op1=ALU.add)
                    else:
                        nc.scalar.copy(out=ds.rearrange("p c i j -> p c j i"), in_=sr.rearrange("p c i j -> p c j i"))
            wgt[i] = wg
            if s == 0:
                later_loads(i)

        def quant(i):
            codes[i] = cpool.tile([P, 2, PW], U32, name="codes", tag="codes", align_bytes=64)
            csc[i] = cpool.tile([P, 2, PW], U8, name="csc", tag="csc", align_bytes=64)
            nc.vector.quantize_mx(
                out=codes[i][:].rearrange("p g w -> p (g w)").bitcast(FP8X4),
                scales=csc[i][:].rearrange("p g w -> p (g w)"),
                in_=wgt[i][:].rearrange("p g w j -> p (g w j)"),
            )

        def mx(i, halves=(0, 1)):
            ci = i
            s, c, sub = ORDER[i]
            c0 = 0
            got = accs.setdefault(i, [])
            for half in halves:
                acc = psum.tile([P, 512], F32, name="acc", tag="acc", bufs=BANKS["acc"])
                if c < 2:
                    h0 = c0 + half * P
                    for g in range(2):
                        nc.tensor.matmul_mx(
                            out=acc[:],
                            lhsT=codes[ci][:, g, h0 : h0 + P].bitcast(FP8X4), lhsT_scale=csc[ci][:, g, h0 : h0 + P],
                            rhs=xq[s][:, g, :].bitcast(FP8X4), rhs_scale=xsc[s][:, g, :],
                            start=(g == 0), stop=(g == 1),
                        )
                else:
                    for t in range(2):
                        t0 = (2 * half + t) * P
                        for g in range(2):
                            nc.tensor.matmul_mx(
                                out=acc[:, t * PW : (t + 1) * PW],
                                lhsT=xq[s][:, g, t0 : t0 + P].bitcast(FP8X4), lhsT_scale=xsc[s][:, g, t0 : t0 + P],
                                rhs=codes[ci][:, g, c0 : c0 + PW].bitcast(FP8X4), rhs_scale=csc[ci][:, g, c0 : c0 + PW],
                                start=(g == 0), stop=(g == 1),
                            )
                got.append(acc)

        def v_out(i):
            s, c, sub = ORDER[i]
            for b in range(2):
                vo = outp.tile([P, 2, 2, P], F32, name="vo", tag="vo")
                nc.vector.tensor_tensor(
                    out=vo[:].rearrange("p h t d -> p t h d"), in0=accs[i][b][:].rearrange("p (t h d) -> p t h d", t=2, h=2),
                    in1=bv[s][:, sub * PW : (sub + 1) * PW].rearrange("p (h d) -> p h d", h=2).unsqueeze(1).to_broadcast([P, 2, 2, P]),
                    op=ALU.add,
                )
                store(out_2, b, i, vo)

        def store(out, b, i, tile):
            s, c, sub = ORDER[i]
            nc.sync.dma_start(
                out=out[b, 2 * sub : 2 * sub + 2, s * 256 : (s + 1) * 256, :].rearrange("h (p t) d -> p h (t d)", t=2),
                in_=tile[:].rearrange("p h t d -> p h (t d)"),
            )

        def bias_col(i, half):
            s, c, sub = ORDER[i]
            row = 8 * s + 4 * c + sub
            return cst[:, half, row : row + 1]

        sqs = {}
        uws = {}
        sqts = {}
        rots = {}
        invs = {}

        def squares(i):
            got = []
            for half in range(2):
                sq = work.tile([P, 512], F32, name="sq", tag="sq")
                nc.scalar.activation(out=sq[:], in_=accs[i][half][:], func=ACT.Square, bias=bias_col(i, half), scale=1.0)
                got.append(sq)
            sqs[i] = got

        def products(i):
            s, c, sub = ORDER[i]
            got = []
            for half in range(2):
                uw = work.tile([P, 2, 512], F32, name="uw", tag="uw")
                for b in range(2):
                    cols = slice(b * 256, (b + 1) * 256)
                    nc.vector.scalar_tensor_tensor(
                        out=uw[:, :, cols], in0=accs[i][half][:, cols].unsqueeze(1).to_broadcast([P, 2, 256]), scalar=bias_col(i, half),
                        in1=tab[:, 2 * s + c, half, :, :], op0=ALU.add, op1=ALU.mult,
                    )
                got.append(uw)
            uws[i] = got

        def turn_squares(i):
            sqt = psum.tile([P, 4, P], F32, name="sqt", tag="sqt", bufs=BANKS["sqt"])
            for tt in range(4):
                for half in range(2):
                    nc.tensor.matmul(
                        out=sqt[:, tt, :], lhsT=sqs[i][half][:, tt * P : (tt + 1) * P], rhs=ident[:],
                        start=(half == 0), stop=(half == 1), is_transpose=True,
                    )
            sqts[i] = sqt

        def sums(i):
            ssum = small.tile([P, 8], F32, name="ssum", tag="ssum")
            nc.vector.tensor_reduce(
                out=ssum[:].rearrange("p (t h) -> p t h", h=2), in_=sqts[i][:].rearrange("p t (c h i) -> p t h c i", h=2, i=RUN),
                axis=mybir.AxisListType.XY, op=ALU.add,
            )
            inv = small.tile([P, 8], F32, name="inv", tag="inv")
            nc.scalar.activation(out=inv[:], in_=ssum[:], func=ACT.Abs_reciprocal_sqrt, bias=epst[:, 0:1], scale=1.0 / 128.0)
            invs[i] = inv

        def rotate(i, bats=(0, 1)):
            got = rots.setdefault(i, [])
            for b in bats:
                rot = psum.tile([P, 2, 2, P], F32, name="rot", tag="rot", bufs=BANKS["rot"])
                for t in range(2):
                    tok = (2 * b + t) * P
                    for r in range(2):
                        for half in range(2):
                            nc.tensor.matmul(
                                out=rot[:, t, r, :], lhsT=uws[i][half][:, r, tok : tok + P], rhs=ident[:],
                                start=(half == 0), stop=(half == 1), is_transpose=True,
                            )
                got.append(rot)

        def finish(i):
            s, c, sub = ORDER[i]
            for b in range(2):
                ot = outp.tile([P, 2, 2, P], F32, name="ot", tag="ot")
                for h in range(2):
                    for t in range(2):
                        nc.scalar.activation(
                            out=ot[:, h, t, :].rearrange("p (c i) -> p c i", i=RUN),
                            in_=rots[i][b][:, t, :, :].rearrange("p r (c h i) -> p h (r c) i", h=2, i=RUN)[:, h, :, :], func=ACT.Copy,
                            scale=invs[i][:, 4 * b + 2 * t + h : 4 * b + 2 * t + h + 1],
                        )
                store(outs[c], b, i, ot)

        def is_piece(i):
            return 0 <= i < PIECES

        def is_qk(i):
            return is_piece(i) and ORDER[i][1] < 2

        ctx.enter_context(tc.manual_schedule(engines={mybir.EngineType.PE}))
        for tau in range(-4, PIECES + 1):
            if is_qk(tau):
                squares(tau)
            if is_qk(tau - 1):
                sums(tau - 1)
                rotate(tau - 1, (0,))
            if is_piece(tau + 1):
                mx(tau + 1, (0,))
            if is_qk(tau - 1):
                rotate(tau - 1, (1,))
            if is_qk(tau):
                products(tau)
            elif is_piece(tau):
                v_out(tau)
            if is_piece(tau + 1):
                mx(tau + 1, (1,))
            if is_qk(tau):
                turn_squares(tau)
            if is_qk(tau - 1):
                finish(tau - 1)
            if tau == -1:
                prep_x(1, ("rot", "rot"))
            if is_piece(tau + 2):
                quant(tau + 2)
            if is_piece(tau + 3):
                inter(tau + 3)
            if is_piece(tau + 4):
                widen(tau + 4)
